import numpy as np
import ml_dtypes


def mxq(x, axis, fmt="e4m3"):
    dtype, down = {"e4m3": (ml_dtypes.float8_e4m3fn, 7), "e5m2": (ml_dtypes.float8_e5m2, 14)}[fmt]
    v = np.moveaxis(np.asarray(x, np.float32).astype(ml_dtypes.bfloat16).astype(np.float64), axis, -1)
    blocks = v.reshape(v.shape[:-1] + (-1, 32))
    amax = np.abs(blocks).max(-1, keepdims=True)
    byte = np.maximum(np.where(amax > 0, np.frexp(amax)[1] - 1 + 127, 0) - down, 1)
    scale = np.exp2(byte - 127.0)
    codes = (blocks / scale).astype(np.float32).astype(dtype).astype(np.float64)
    return np.moveaxis((codes * scale).reshape(v.shape), -1, axis)


WIDE = False


def mx_kscale(k):
    if not WIDE:
        return np.ones(k)
    levels = np.array([18, -18])
    if k % 512:
        return np.exp2(np.random.permutation(np.resize(levels, k // 32))).repeat(32)
    a = np.empty((k // 512, 16))
    for p in range(k // 512):
        a[p, :8] = np.random.permutation(np.resize(levels, 8))
        for g in range(8):
            far = levels[np.abs(levels - a[p, g]) >= 10]
            a[p, g + 8] = far[np.random.randint(len(far))]
    return np.exp2(a.ravel()).repeat(32)


BF16 = ml_dtypes.bfloat16


def bf(x):
    return np.asarray(x, np.float32).astype(BF16)


def f64(x):
    return np.asarray(x).astype(np.float64)


B, N, F, H = 512, 5, 512, 1024
M = N - 1


def setup_inputs():
    s = mx_kscale(B * M)[::M][:, None]
    u = mx_kscale(F)
    v = mx_kscale(H)
    w1a = np.random.standard_normal((H, F)) / np.sqrt(F * M)
    w1b = np.random.standard_normal((H, F)) / np.sqrt(F)
    x_0 = bf(np.random.standard_normal((B, N, F)))
    W1_0 = bf(np.concatenate([w1a, w1b], axis=1))
    W2_0 = bf(np.random.standard_normal((F, H)) / np.sqrt(H * M))
    W0_0 = bf(np.random.standard_normal((F, F)) / np.sqrt(F))
    g = bf(4.0 * np.random.standard_normal((B, F)) * np.exp2(np.random.randint(-6, 1, (B, 1))) / s * u)
    h0 = f64(x_0)[:, 0, :] @ f64(W1_0)[:, :F].T
    hi = f64(x_0)[:, 1:, :] @ f64(W1_0)[:, F:].T
    t = np.tanh(h0[:, None, :] + hi)
    return {"x": bf(f64(x_0) * s[:, :, None]),
            "W1": bf(f64(W1_0) / v[:, None]),
            "W2": bf(f64(W2_0) * v / u[:, None]),
            "W0": bf(f64(W0_0) / u[:, None]),
            "interact": np.asarray(t, np.float32),
            "grad_out": g}


def reference(x, W1, W2, W0, interact, grad_out):
    xf = f64(x)
    anchor = np.repeat(xf[:, :1, :], M, axis=1)
    cat = np.concatenate([anchor, xf[:, 1:, :]], axis=2).reshape(B * M, 2 * F)
    Wc = np.concatenate([f64(W2), f64(W0)], axis=1)
    d = mxq(f64(grad_out), 1, "e5m2") @ mxq(Wc, 0, "e4m3")
    dh = d[:, :H]
    skip = d[:, H:]
    t = f64(interact)
    dz1 = (dh[:, None, :] * (1.0 - t * t)).reshape(B * M, H)
    dcat = mxq(dz1, 1, "e5m2") @ mxq(f64(W1), 0, "e4m3")
    dW1 = mxq(dz1, 0, "e5m2").T @ mxq(cat, 0, "e4m3")
    dcat = dcat.reshape(B, M, 2 * F)
    dx0 = skip + dcat[:, :, :F].sum(axis=1)
    dx = np.concatenate([dx0[:, None, :], dcat[:, :, F:]], axis=1)
    return dx, dW1

@@ -1,0 +1,300 @@
+from contextlib import ExitStack
+
+import concourse.mybir as mybir
+from concourse.masks import make_identity
+
+B, NB, F, H = 512, 4, 512, 1024
+P = 128
+PACK = 4
+KP = P * PACK
+G = B // P
+HH = H // KP
+HALF = KP * NB // 2
+
+F32 = mybir.dt.float32
+BF16 = mybir.dt.bfloat16
+U32 = mybir.dt.uint32
+U8 = mybir.dt.uint8
+E4 = mybir.dt.float8_e4m3fn_x4
+E5 = mybir.dt.float8_e5m2_x4
+ALU = mybir.AluOpType
+ACT = mybir.ActivationFunctionType
+
+ROW_BUFS = 7
+TANH_BUFS = 5
+DZ_BUFS = 8
+B_BUFS = 8
+RES_BUFS = 6
+LOADS = ("w20", "grad0", "t0", "w21", "t1", "w1n0", "w1n1", "t2", "w1a0", "w1a1", "t3", "w0", "grad1", "t4")
+ORDER = "l:t5 f:1 l:t6 b:0:SS i:w1n0:V i:w1n1:S f:2 l:t7 l:xn0 l:xn1 l:xn2 l:xn3 l:xa0 l:xa1 l:xa2 l:xa3 b:1:SS i:w1a0:V i:w1a1:S i:w0:V g f:3 b:2:SS r:0:SSSSS f:4 b:3:SS f:5 r:1:SSSSS b:4:SS f:6 b:5:SS f:7 r:2:SSSSS b:6:SS b:7:SS i:a0:V i:xn0:V r:3:SSSSS i:a2:V i:xn1:V i:a4:V i:xn2:S i:a6:V i:xn3:V w:0:n:0:SSSS i:xa0:V i:xa1:S i:xa2:V i:xa3:V w:0:a:4:SSSS i:a1:S i:a3:V i:a5:S i:a7:V w:1:n:0:VSVS w:1:a:4:VSVS"
+
+FLOPS = 2 * B * F * (H + F) + 2 * 2 * B * NB * H * 2 * F
+
+
+def tile_attention_pa_v_kernel(tc, x, W1, W2, W0, interact, grad_out, out_0, out_1):
+    nc = tc.nc
+    with ExitStack() as ctx:
+        sb = ctx.enter_context(tc.tile_pool(name="sb", bufs=1))
+        psum = ctx.enter_context(tc.psum_pool(name="psum", bufs=1))
+
+        ident = sb.tile([P, P], F32, name="ident")
+        make_identity(nc, ident[:])
+
+        raw, staged, mx, squares, dhs, dz, banks, accs = {}, {}, {}, {}, {}, {}, {}, {}
+
+        w2_rows = W2.rearrange("(p j) h -> p j h", j=PACK)
+        w1_rows = W1.rearrange("(h p j) f -> h p j f", h=HH, j=PACK)
+        sources = {"w0": W0.rearrange("(p j) f -> p j f", j=PACK)}
+        for h in range(HH):
+            sources["w2%d" % h] = w2_rows[:, :, h * KP:(h + 1) * KP]
+            sources["w1a%d" % h] = w1_rows[h, :, :, 0:F]
+            sources["w1n%d" % h] = w1_rows[h, :, :, F:2 * F]
+        for g in range(G):
+            sources["xn%d" % g] = x[g * P:(g + 1) * P, 1:, :]
+
+        def load_rows(key):
+            t = sb.tile([P, PACK, KP], BF16, name="raw_" + key, tag="rows", bufs=ROW_BUFS, align_bytes=64)
+            nc.sync.dma_start(out=t[:], in_=sources[key])
+            raw[key] = t
+
+        def load_anchor(g):
+            t = sb.tile([P, F], BF16, name="raw_xa%d" % g, align_bytes=64)
+            nc.sync.dma_start(out=t[:], in_=x[g * P:(g + 1) * P, 0, :])
+            raw["xa%d" % g] = t
+
+        def load_grad(pair):
+            t = sb.tile([P, 2, F], BF16, name="raw_grad%d" % pair, align_bytes=64)
+            nc.sync.dma_start(out=t[:], in_=grad_out[2 * pair * P:2 * (pair + 1) * P].rearrange("(g p) f -> p g f", p=P))
+            raw["grad%d" % pair] = t
+
+        def load_tanh(k):
+            g, h = divmod(k, HH)
+            t = sb.tile([P, NB, KP], F32, name="raw_t%d" % k, tag="tanh", bufs=TANH_BUFS, align_bytes=64)
+            nc.sync.dma_start(out=t[:], in_=interact[g * P:(g + 1) * P, :, h * KP:(h + 1) * KP])
+            raw["t%d" % k] = t
+
+        def stage(key, tag="stage", bufs=3, width=KP * PACK):
+            t = sb.tile([P, width], BF16, name="st_" + key, tag=tag, bufs=bufs, align_bytes=64)
+            staged[key] = t
+            return t
+
+        def quantize(key, fmt, tag=None, bufs=1):
+            src = staged[key]
+            width = src.shape[1] // PACK
+            codes = sb.tile([P, width], U32, name="c_" + key, tag=(tag or key) + "_c", bufs=bufs, align_bytes=64)
+            scales = sb.tile([P, width], U8, name="s_" + key, tag=(tag or key) + "_s", bufs=bufs, align_bytes=64)
+            nc.vector.quantize_mx(out=codes[:].bitcast(fmt), scales=scales[:], in_=src[:])
+            mx[key] = (codes, scales, fmt)
+
+        def mm(out, lkey, block, rkey, start, stop):
+            lc, ls, lf = mx[lkey]
+            rc, rs, rf = mx[rkey]
+            cols = slice(block * P, (block + 1) * P)
+            nc.tensor.matmul_mx(out=out[:], lhsT=lc[:, cols].bitcast(lf), lhsT_scale=ls[:, cols],
+                                rhs=rc[:].bitcast(rf), rhs_scale=rs[:], start=start, stop=stop)
+
+        def copy_on(engine, out, in_):
+            if engine == "S":
+                nc.scalar.copy(out=out, in_=in_)
+            else:
+                nc.vector.tensor_copy(out=out, in_=in_)
+
+        def weave(key, engine):
+            st = stage(key)
+            copy_on(engine, st[:].rearrange("p (c i j) -> p c j i", i=4, j=PACK),
+                    raw[key][:].rearrange("p j (c i) -> p c j i", i=4))
+
+        def weave_w2(h):
+            key = "w2%d" % h
+            st = stage(key)
+            for u in range(2):
+                nc.vector.tensor_scalar(
+                    out=st[:, u * HALF:(u + 1) * HALF].rearrange("p (w e j) -> p w j e", e=2, j=PACK),
+                    in0=raw[key][:].rearrange("p j (w u e) -> p u w j e", u=2, e=2)[:, u],
+                    scalar1=-1.0, scalar2=None, op0=ALU.mult)
+
+        def weave_anchor(g, engine):
+            key = "xa%d" % g
+            st = stage(key)
+            copy_on(engine, st[:].rearrange("p (c j) -> p c j", j=PACK),
+                    raw[key][:].unsqueeze(2).to_broadcast([P, F, PACK]))
+
+        def weave_dz(k, engine):
+            st = stage("a%d" % k)
+            copy_on(engine, st[:].rearrange("p (u e w i) -> p u w i e", u=2, e=2, i=NB),
+                    dz[k][:].rearrange("p (u i w e) -> p u w i e", u=2, i=NB, e=2))
+
+        def turn_grad(pair, engine):
+            words = raw["grad%d" % pair][:].rearrange("p g f -> p (g f)").bitcast(F32)
+            st = stage("grad%d" % pair, tag="gstage", bufs=2, width=HALF)
+            bank = psum.tile([P, 4, P], F32, name="gtr", tag="bank%d" % (1 + pair))
+            for n in range(4):
+                g, u = divmod(n, 2)
+                nc.tensor.transpose(bank[:, n, :], words[:, 256 * g + u:256 * (g + 1):2], ident[:])
+            copy_on(engine, st[:].bitcast(F32).rearrange("p (g b u) -> p g b u", g=2, u=2),
+                    bank[:].rearrange("p (g u) b -> p g b u", u=2))
+
+        def square(k):
+            sq = sb.tile([P, KP * NB], F32, name="sq%d" % k, tag="sq", bufs=2, align_bytes=64)
+            nc.scalar.activation(
+                out=sq[:].rearrange("p (u n e) -> p n u e", u=2, e=2),
+                in_=raw["t%d" % k][:].rearrange("p i (w u e) -> p (i w) u e", u=2, e=2),
+                func=ACT.Square)
+            squares[k] = sq
+
+        def dh_product(k):
+            g, h = divmod(k, HH)
+            dh = psum.tile([P, KP], F32, name="dh%d" % k, tag="bank0")
+            mm(dh, "grad%d" % (g // 2), g % 2, "w2%d" % h, True, True)
+            dhs[k] = dh
+
+        def make_dz(k):
+            z = sb.tile([P, KP * NB], BF16, name="dz%d" % k, tag="dz", bufs=DZ_BUFS, align_bytes=64)
+            for u in range(2):
+                part = slice(u * HALF, (u + 1) * HALF)
+                nc.vector.scalar_tensor_tensor(
+                    out=z[:, part].rearrange("p (i c) -> p i c", i=NB),
+                    in0=squares[k][:, part].rearrange("p (i c) -> p i c", i=NB), scalar=1.0,
+                    in1=dhs[k][:, u * 256:(u + 1) * 256].unsqueeze(1).to_broadcast([P, NB, 256]),
+                    op0=ALU.subtract, op1=ALU.mult)
+            dz[k] = z
+
+        def turn_dz(k):
+            words = dz[k][:].bitcast(F32).rearrange("p (u i w) -> p u i w", u=2, i=NB)
+            for pair in range(2):
+                bank = psum.tile([P, 4, P], F32, name="tr%d%d" % (k, pair), tag="bank%d" % (1 + pair))
+                for n in range(4):
+                    i, u = divmod(n, 2)
+                    nc.tensor.transpose(bank[:, n, :], words[:, u, 2 * pair + i, :], ident[:])
+                banks[k, pair] = bank
+
+        def fetch_dz(k, pair, engine):
+            st = stage("b%d%d" % (k, pair), tag="bstage", bufs=3, width=HALF)
+            copy_on(engine, st[:].bitcast(F32).rearrange("p (i b u) -> p i b u", i=2, u=2),
+                    banks[k, pair][:].rearrange("p (i u) b -> p i b u", u=2))
+
+        def quantize_b(k, pair):
+            quantize("b%d%d" % (k, pair), E5, tag="b", bufs=B_BUFS)
+
+        def new_acc(key, bank):
+            acc = psum.tile([P, KP], F32, name="acc_" + key, tag="bank%d" % bank)
+            accs[key] = acc
+            return acc
+
+        def emit(key, dst, engine):
+            res = sb.tile([P, KP], F32, name="res_" + key, tag="res", bufs=RES_BUFS)
+            copy_on(engine, res[:], accs[key][:])
+            nc.sync.dma_start(out=dst, in_=res[:])
+
+        def dx_neighbour(g, i):
+            acc = new_acc("n%d%d" % (g, i), 3 + i)
+            for h in range(HH):
+                mm(acc, "b%d%d" % (HH * g + h, i // 2), i % 2, "w1n%d" % h, h == 0, h == HH - 1)
+
+        def emit_neighbour(g, i, engine):
+            emit("n%d%d" % (g, i), out_0[g * P:(g + 1) * P, 1 + i, :], engine)
+
+        def dx_anchor(g):
+            acc = new_acc("a%d" % g, 7)
+            mm(acc, "grad%d" % (g // 2), g % 2, "w0", True, False)
+            for h in range(HH):
+                for i in range(NB):
+                    mm(acc, "b%d%d" % (HH * g + h, i // 2), i % 2, "w1a%d" % h, False, h == HH - 1 and i == NB - 1)
+
+        def emit_anchor(g, engine):
+            emit("a%d" % g, out_0[g * P:(g + 1) * P, 0, :], engine)
+
+        dw_rows = out_1.rearrange("(h m t) f -> h t m f", h=HH, t=PACK)
+
+        def dw_pass(h, side, t, g, bank):
+            key = "w%d%s%d" % (h, side, t)
+            if g == 0:
+                new_acc(key, bank)
+            mm(accs[key], "a%d" % (HH * g + h), t, "x%s%d" % (side, g), g == 0, g == G - 1)
+
+        def emit_dw(h, side, t, engine):
+            first = 0 if side == "a" else F
+            emit("w%d%s%d" % (h, side, t), dw_rows[h, t, :, first:first + F], engine)
+
+        def prepare(key, engine):
+            if key[0] == "a":
+                weave_dz(int(key[1]), engine)
+            elif key[:2] == "xa":
+                weave_anchor(int(key[2]), engine)
+            else:
+                weave(key, engine)
+
+        def finish(key):
+            quantize(key, E5 if key[0] == "a" else E4)
+
+
+        for key in LOADS:
+            if key[0] == "w" or key[:2] == "xn":
+                load_rows(key)
+            elif key[0] == "g":
+                load_grad(int(key[-1]))
+            elif key[0] == "x":
+                load_anchor(int(key[-1]))
+            else:
+                load_tanh(int(key[-1]))
+
+        def item(key, engine):
+            prepare(key, engine)
+            finish(key)
+
+        def front(k):
+            square(k)
+            dh_product(k)
+            make_dz(k)
+
+        def back(k, e0, e1):
+            turn_dz(k)
+            fetch_dz(k, 0, e0)
+            quantize_b(k, 0)
+            fetch_dz(k, 1, e1)
+            quantize_b(k, 1)
+
+        def rows(g, engines):
+            for i in range(NB):
+                dx_neighbour(g, i)
+                emit_neighbour(g, i, engines[i])
+            dx_anchor(g)
+            emit_anchor(g, engines[4])
+
+        def block(h, side, first, engines):
+            for t in range(PACK):
+                for g in range(G):
+                    dw_pass(h, side, t, g, first + t)
+                emit_dw(h, side, t, engines[t])
+
+        weave_w2(0)
+        turn_grad(0, "S")
+        quantize("w20", E4)
+        quantize("grad0", E5)
+        front(0)
+        weave_w2(1)
+        quantize("w21", E4)
+        for step in ORDER.split():
+            a = step.split(":")
+            if a[0] == "f":
+                front(int(a[1]))
+            elif a[0] == "b":
+                back(int(a[1]), a[2][0], a[2][1])
+            elif a[0] == "i":
+                item(a[1], a[2])
+            elif a[0] == "q":
+                finish(a[1])
+            elif a[0] == "r":
+                rows(int(a[1]), a[2])
+            elif a[0] == "g":
+                turn_grad(1, "S")
+                quantize("grad1", E5)
+            elif a[0] == "l":
+                if a[1][0] == "t":
+                    load_tanh(int(a[1][1]))
+                elif a[1][1] == "n":
+                    load_rows(a[1])
+                else:
+                    load_anchor(int(a[1][2]))
+            else:
+                block(int(a[1]), a[2], int(a[3]), a[4])

@@ -7,9 +7,14 @@ B, NB, F, H = 512, 4, 512, 1024
 P = 128
 PACK = 4
 KP = P * PACK
-G = B // P
-HH = H // KP
-HALF = KP * NB // 2
+WIDE = KP * PACK
+HALF = WIDE // 2
+BLOCKS = B // P
+HALVES = H // KP
+CHUNKS = BLOCKS * HALVES
+
+DH_BANK, TURN_BANK, DX_BANK = 0, 1, 3
+DW_BANKS = {"n": 0, "a": 4}
 
 F32 = mybir.dt.float32
 BF16 = mybir.dt.bfloat16
@@ -19,14 +24,7 @@ E4 = mybir.dt.float8_e4m3fn_x4
 E5 = mybir.dt.float8_e5m2_x4
 ALU = mybir.AluOpType
 ACT = mybir.ActivationFunctionType
-
-ROW_BUFS = 7
-TANH_BUFS = 5
-DZ_BUFS = 8
-B_BUFS = 8
-RES_BUFS = 6
-LOADS = ("w20", "grad0", "t0", "w21", "t1", "w1n0", "w1n1", "t2", "w1a0", "w1a1", "t3", "w0", "grad1", "t4")
-ORDER = "l:t5 f:1 l:t6 b:0:SS i:w1n0:V i:w1n1:S f:2 l:t7 l:xn0 l:xn1 l:xn2 l:xn3 l:xa0 l:xa1 l:xa2 l:xa3 b:1:SS i:w1a0:V i:w1a1:S i:w0:V g f:3 b:2:SS r:0:SSSSS f:4 b:3:SS f:5 r:1:SSSSS b:4:SS f:6 b:5:SS f:7 r:2:SSSSS b:6:SS b:7:SS i:a0:V i:xn0:V r:3:SSSSS i:a2:V i:xn1:V i:a4:V i:xn2:S i:a6:V i:xn3:V w:0:n:0:SSSS i:xa0:V i:xa1:S i:xa2:V i:xa3:V w:0:a:4:SSSS i:a1:S i:a3:V i:a5:S i:a7:V w:1:n:0:VSVS w:1:a:4:VSVS"
+SCALAR, VECTOR = "scalar", "vector"
 
 FLOPS = 2 * B * F * (H + F) + 2 * 2 * B * NB * H * 2 * F
 
@@ -36,265 +34,321 @@ def tile_attention_pa_v_kernel(tc, x, W1, W2, W0, interact, grad_out, out_0, out
     with ExitStack() as ctx:
         sb = ctx.enter_context(tc.tile_pool(name="sb", bufs=1))
         psum = ctx.enter_context(tc.psum_pool(name="psum", bufs=1))
+        ctx.enter_context(tc.manual_schedule())
 
         ident = sb.tile([P, P], F32, name="ident")
         make_identity(nc, ident[:])
 
-        raw, staged, mx, squares, dhs, dz, banks, accs = {}, {}, {}, {}, {}, {}, {}, {}
+        raw, woven, mx = {}, {}, {}
+        tanh, squares, neg_dh, dz, turned, sums = {}, {}, {}, {}, {}, {}
 
-        w2_rows = W2.rearrange("(p j) h -> p j h", j=PACK)
-        w1_rows = W1.rearrange("(h p j) f -> h p j f", h=HH, j=PACK)
-        sources = {"w0": W0.rearrange("(p j) f -> p j f", j=PACK)}
-        for h in range(HH):
-            sources["w2%d" % h] = w2_rows[:, :, h * KP:(h + 1) * KP]
-            sources["w1a%d" % h] = w1_rows[h, :, :, 0:F]
-            sources["w1n%d" % h] = w1_rows[h, :, :, F:2 * F]
-        for g in range(G):
-            sources["xn%d" % g] = x[g * P:(g + 1) * P, 1:, :]
+        def bank(name, number, shape):
+            return psum.tile(shape, F32, name=name, tag="bank%d" % number)
 
-        def load_rows(key):
-            t = sb.tile([P, PACK, KP], BF16, name="raw_" + key, tag="rows", bufs=ROW_BUFS, align_bytes=64)
-            nc.sync.dma_start(out=t[:], in_=sources[key])
-            raw[key] = t
+        def load_rows(name, source):
+            t = sb.tile([P] + list(source.shape[1:]), BF16, name="raw_" + name, tag="rows", bufs=4, align_bytes=64)
+            nc.sync.dma_start(out=t[:], in_=source)
+            return t
 
-        def load_anchor(g):
-            t = sb.tile([P, F], BF16, name="raw_xa%d" % g, align_bytes=64)
-            nc.sync.dma_start(out=t[:], in_=x[g * P:(g + 1) * P, 0, :])
-            raw["xa%d" % g] = t
+        def load_w2():
+            t = load_rows("w2", W2.rearrange("(p j) h -> p j h", j=PACK))
+            for s in range(HALVES):
+                raw["w2%d" % s] = t[:, :, s * KP:(s + 1) * KP]
+
+        def load_w0():
+            raw["w0"] = load_rows("w0", W0.rearrange("(p j) f -> p j f", j=PACK))[:]
+
+        def load_w1(s):
+            t = load_rows("w1%d" % s, W1.rearrange("(s p j) f -> s p j f", s=HALVES, j=PACK)[s])
+            raw["w1a%d" % s], raw["w1n%d" % s] = t[:, :, 0:F], t[:, :, F:2 * F]
+
+        def load_x(g):
+            t = load_rows("x%d" % g, x[g * P:(g + 1) * P])
+            raw["xn%d" % g] = t[:, 1:, :]
+            raw["xa%d" % g] = t[:, 0, :]
 
         def load_grad(pair):
             t = sb.tile([P, 2, F], BF16, name="raw_grad%d" % pair, align_bytes=64)
-            nc.sync.dma_start(out=t[:], in_=grad_out[2 * pair * P:2 * (pair + 1) * P].rearrange("(g p) f -> p g f", p=P))
+            rows = grad_out[2 * pair * P:2 * (pair + 1) * P]
+            nc.sync.dma_start(out=t[:], in_=rows.rearrange("(g p) f -> p g f", p=P))
             raw["grad%d" % pair] = t
 
-        def load_tanh(k):
-            g, h = divmod(k, HH)
-            t = sb.tile([P, NB, KP], F32, name="raw_t%d" % k, tag="tanh", bufs=TANH_BUFS, align_bytes=64)
-            nc.sync.dma_start(out=t[:], in_=interact[g * P:(g + 1) * P, :, h * KP:(h + 1) * KP])
-            raw["t%d" % k] = t
+        def load_tanh(c):
+            g, s = divmod(c, HALVES)
+            t = sb.tile([P, NB, KP], F32, name="tanh%d" % c, tag="tanh", bufs=4, align_bytes=64)
+            nc.sync.dma_start(out=t[:], in_=interact[g * P:(g + 1) * P, :, s * KP:(s + 1) * KP])
+            tanh[c] = t
 
-        def stage(key, tag="stage", bufs=3, width=KP * PACK):
-            t = sb.tile([P, width], BF16, name="st_" + key, tag=tag, bufs=bufs, align_bytes=64)
-            staged[key] = t
+        def new_woven(name, tag="woven", bufs=4, width=WIDE):
+            t = sb.tile([P, width], BF16, name="woven_" + name, tag=tag, bufs=bufs, align_bytes=64)
+            woven[name] = t
             return t
 
-        def quantize(key, fmt, tag=None, bufs=1):
-            src = staged[key]
-            width = src.shape[1] // PACK
-            codes = sb.tile([P, width], U32, name="c_" + key, tag=(tag or key) + "_c", bufs=bufs, align_bytes=64)
-            scales = sb.tile([P, width], U8, name="s_" + key, tag=(tag or key) + "_s", bufs=bufs, align_bytes=64)
-            nc.vector.quantize_mx(out=codes[:].bitcast(fmt), scales=scales[:], in_=src[:])
-            mx[key] = (codes, scales, fmt)
-
-        def mm(out, lkey, block, rkey, start, stop):
-            lc, ls, lf = mx[lkey]
-            rc, rs, rf = mx[rkey]
-            cols = slice(block * P, (block + 1) * P)
-            nc.tensor.matmul_mx(out=out[:], lhsT=lc[:, cols].bitcast(lf), lhsT_scale=ls[:, cols],
-                                rhs=rc[:].bitcast(rf), rhs_scale=rs[:], start=start, stop=stop)
-
-        def copy_on(engine, out, in_):
-            if engine == "S":
+        def copy(engine, out, in_):
+            if engine == SCALAR:
                 nc.scalar.copy(out=out, in_=in_)
             else:
                 nc.vector.tensor_copy(out=out, in_=in_)
 
-        def weave(key, engine):
-            st = stage(key)
-            copy_on(engine, st[:].rearrange("p (c i j) -> p c j i", i=4, j=PACK),
-                    raw[key][:].rearrange("p j (c i) -> p c j i", i=4))
+        def weave(name, engine):
+            copy(engine, new_woven(name)[:].rearrange("p (n r j) -> p n j r", r=4, j=PACK),
+                 raw[name].rearrange("p j (n r) -> p n j r", r=4))
 
-        def weave_w2(h):
-            key = "w2%d" % h
-            st = stage(key)
-            for u in range(2):
-                nc.vector.tensor_scalar(
-                    out=st[:, u * HALF:(u + 1) * HALF].rearrange("p (w e j) -> p w j e", e=2, j=PACK),
-                    in0=raw[key][:].rearrange("p j (w u e) -> p u w j e", u=2, e=2)[:, u],
-                    scalar1=-1.0, scalar2=None, op0=ALU.mult)
+        def side_by_side(name):
+            if name.startswith("xa"):
+                return raw[name].unsqueeze(2).to_broadcast([P, F, NB])
+            return raw[name].rearrange("p j n -> p n j")
 
         def weave_anchor(g, engine):
-            key = "xa%d" % g
-            st = stage(key)
-            copy_on(engine, st[:].rearrange("p (c j) -> p c j", j=PACK),
-                    raw[key][:].unsqueeze(2).to_broadcast([P, F, PACK]))
+            name = "xa%d" % g
+            copy(engine, new_woven(name)[:].rearrange("p (n j) -> p n j", j=PACK), side_by_side(name))
 
-        def weave_dz(k, engine):
-            st = stage("a%d" % k)
-            copy_on(engine, st[:].rearrange("p (u e w i) -> p u w i e", u=2, e=2, i=NB),
-                    dz[k][:].rearrange("p (u i w e) -> p u w i e", u=2, i=NB, e=2))
+        def weave_on_gpsimd(name):
+            t = new_woven(name, tag="gpsimd", bufs=1)
+            nc.gpsimd.tensor_scalar(out=t[:].rearrange("p (n j) -> p n j", j=PACK),
+                                    in0=side_by_side(name),
+                                    scalar1=1.0, scalar2=0.0, op0=ALU.mult, op1=ALU.add)
 
-        def turn_grad(pair, engine):
+        def weave_w2(s, tag, bufs):
+            name = "w2%d" % s
+            t = new_woven(name, tag=tag, bufs=bufs)
+            for u in range(2):
+                nc.vector.tensor_scalar(
+                    out=t[:, u * HALF:(u + 1) * HALF].rearrange("p (w e j) -> p w j e", e=2, j=PACK),
+                    in0=raw[name].rearrange("p j (w u e) -> p u w j e", u=2, e=2)[:, u],
+                    scalar1=-1.0, scalar2=None, op0=ALU.mult)
+
+        def weave_tokens(c, engine):
+            copy(engine, new_woven("tok%d" % c)[:].rearrange("p (u e w i) -> p u w i e", u=2, e=2, i=NB),
+                 dz[c][:].rearrange("p (u i w e) -> p u w i e", u=2, i=NB, e=2))
+
+        def quantize(name):
+            src = woven[name]
+            words = src.shape[1] // PACK
+            fmt = E4 if name[0] in "wx" else E5
+            tag, bufs = ("feat", 4) if name.startswith("feat") else (name, 1)
+            codes = sb.tile([P, words], U32, name="codes_" + name, tag=tag + "_codes", bufs=bufs, align_bytes=64)
+            scales = sb.tile([P, words], U8, name="scales_" + name, tag=tag + "_scales", bufs=bufs, align_bytes=64)
+            nc.vector.quantize_mx(out=codes[:].bitcast(fmt), scales=scales[:], in_=src[:])
+            mx[name] = (codes, scales, fmt)
+
+        def mx_pass(out, left, block, right, start, stop):
+            left_codes, left_scales, left_fmt = mx[left]
+            right_codes, right_scales, right_fmt = mx[right]
+            cols = slice(block * P, (block + 1) * P)
+            nc.tensor.matmul_mx(out=out[:], lhsT=left_codes[:, cols].bitcast(left_fmt), lhsT_scale=left_scales[:, cols],
+                                rhs=right_codes[:].bitcast(right_fmt), rhs_scale=right_scales[:], start=start, stop=stop)
+
+        def turn_grad(pair, number):
             words = raw["grad%d" % pair][:].rearrange("p g f -> p (g f)").bitcast(F32)
-            st = stage("grad%d" % pair, tag="gstage", bufs=2, width=HALF)
-            bank = psum.tile([P, 4, P], F32, name="gtr", tag="bank%d" % (1 + pair))
+            t = bank("turn_grad%d" % pair, number, [P, 4, P])
             for n in range(4):
                 g, u = divmod(n, 2)
-                nc.tensor.transpose(bank[:, n, :], words[:, 256 * g + u:256 * (g + 1):2], ident[:])
-            copy_on(engine, st[:].bitcast(F32).rearrange("p (g b u) -> p g b u", g=2, u=2),
-                    bank[:].rearrange("p (g u) b -> p g b u", u=2))
+                nc.tensor.transpose(t[:, n, :], words[:, 2 * P * g + u:2 * P * (g + 1):2], ident[:])
+            turned["grad", pair] = t
 
-        def square(k):
-            sq = sb.tile([P, KP * NB], F32, name="sq%d" % k, tag="sq", bufs=2, align_bytes=64)
-            nc.scalar.activation(
-                out=sq[:].rearrange("p (u n e) -> p n u e", u=2, e=2),
-                in_=raw["t%d" % k][:].rearrange("p i (w u e) -> p (i w) u e", u=2, e=2),
-                func=ACT.Square)
-            squares[k] = sq
+        def fetch_grad(pair):
+            t = new_woven("grad%d" % pair, tag="woven_grad", bufs=2, width=HALF)
+            nc.scalar.copy(out=t[:].bitcast(F32).rearrange("p (g b u) -> p g b u", g=2, u=2),
+                           in_=turned["grad", pair][:].rearrange("p (g u) b -> p g b u", u=2))
 
-        def dh_product(k):
-            g, h = divmod(k, HH)
-            dh = psum.tile([P, KP], F32, name="dh%d" % k, tag="bank0")
-            mm(dh, "grad%d" % (g // 2), g % 2, "w2%d" % h, True, True)
-            dhs[k] = dh
+        def square(c):
+            t = sb.tile([P, WIDE], F32, name="square%d" % c, tag="square", bufs=2, align_bytes=64)
+            nc.scalar.activation(out=t[:], in_=tanh[c][:].rearrange("p i h -> p (i h)"), func=ACT.Square)
+            squares[c] = t
 
-        def make_dz(k):
-            z = sb.tile([P, KP * NB], BF16, name="dz%d" % k, tag="dz", bufs=DZ_BUFS, align_bytes=64)
+        def dh_pass(c, number=DH_BANK):
+            g, s = divmod(c, HALVES)
+            neg_dh[c] = bank("neg_dh%d" % c, number, [P, KP])
+            mx_pass(neg_dh[c], "grad%d" % (g // 2), g % 2, "w2%d" % s, True, True)
+
+        def make_dz(c):
+            t = sb.tile([P, WIDE], BF16, name="dz%d" % c, tag="dz", bufs=CHUNKS, align_bytes=64)
             for u in range(2):
-                part = slice(u * HALF, (u + 1) * HALF)
+                factor = neg_dh[c][:, u * 2 * P:(u + 1) * 2 * P].rearrange("p (w e) -> p w e", e=2)
                 nc.vector.scalar_tensor_tensor(
-                    out=z[:, part].rearrange("p (i c) -> p i c", i=NB),
-                    in0=squares[k][:, part].rearrange("p (i c) -> p i c", i=NB), scalar=1.0,
-                    in1=dhs[k][:, u * 256:(u + 1) * 256].unsqueeze(1).to_broadcast([P, NB, 256]),
+                    out=t[:, u * HALF:(u + 1) * HALF].rearrange("p (i w e) -> p i w e", i=NB, e=2),
+                    in0=squares[c][:].rearrange("p (i w u e) -> p u i w e", i=NB, u=2, e=2)[:, u], scalar=1.0,
+                    in1=factor.unsqueeze(1).to_broadcast([P, NB, P, 2]),
                     op0=ALU.subtract, op1=ALU.mult)
-            dz[k] = z
+            dz[c] = t
 
-        def turn_dz(k):
-            words = dz[k][:].bitcast(F32).rearrange("p (u i w) -> p u i w", u=2, i=NB)
+        def turn_dz(c):
+            words = dz[c][:].bitcast(F32).rearrange("p (u i w) -> p u i w", u=2, i=NB)
             for pair in range(2):
-                bank = psum.tile([P, 4, P], F32, name="tr%d%d" % (k, pair), tag="bank%d" % (1 + pair))
+                t = bank("turn%d_%d" % (c, pair), TURN_BANK + pair, [P, 4, P])
                 for n in range(4):
                     i, u = divmod(n, 2)
-                    nc.tensor.transpose(bank[:, n, :], words[:, u, 2 * pair + i, :], ident[:])
-                banks[k, pair] = bank
+                    nc.tensor.transpose(t[:, n, :], words[:, u, 2 * pair + i, :], ident[:])
+                turned[c, pair] = t
 
-        def fetch_dz(k, pair, engine):
-            st = stage("b%d%d" % (k, pair), tag="bstage", bufs=3, width=HALF)
-            copy_on(engine, st[:].bitcast(F32).rearrange("p (i b u) -> p i b u", i=2, u=2),
-                    banks[k, pair][:].rearrange("p (i u) b -> p i b u", u=2))
+        def fetch_dz(c, pair, engine):
+            name = "feat%d" % c
+            if pair == 0:
+                new_woven(name, tag="woven_feat", bufs=2)
+            part = woven[name][:, pair * HALF:(pair + 1) * HALF]
+            copy(engine, part.bitcast(F32).rearrange("p (i b u) -> p i b u", i=2, u=2),
+                 turned[c, pair][:].rearrange("p (i u) b -> p i b u", u=2))
 
-        def quantize_b(k, pair):
-            quantize("b%d%d" % (k, pair), E5, tag="b", bufs=B_BUFS)
+        def dx_passes(c):
+            g, s = divmod(c, HALVES)
+            last = s == HALVES - 1
+            for i in range(NB):
+                if s == 0:
+                    sums["dx", g, 1 + i] = bank("dx%d_%d" % (g, 1 + i), DX_BANK + i, [P, KP])
+                mx_pass(sums["dx", g, 1 + i], "feat%d" % c, i, "w1n%d" % s, s == 0, last)
+            if s == 0:
+                sums["dx", g, 0] = bank("dx%d_0" % g, DX_BANK + NB, [P, KP])
+                mx_pass(sums["dx", g, 0], "grad%d" % (g // 2), g % 2, "w0", True, False)
+            for i in range(NB):
+                mx_pass(sums["dx", g, 0], "feat%d" % c, i, "w1a%d" % s, False, last and i == NB - 1)
 
-        def new_acc(key, bank):
-            acc = psum.tile([P, KP], F32, name="acc_" + key, tag="bank%d" % bank)
-            accs[key] = acc
-            return acc
+        def dw_pass(s, side, t, g):
+            if g == 0:
+                sums[s, side, t] = bank("dw%d%s%d" % (s, side, t), DW_BANKS[side] + t, [P, KP])
+            mx_pass(sums[s, side, t], "tok%d" % (HALVES * g + s), t, "x%s%d" % (side, g), g == 0, g == BLOCKS - 1)
 
-        def emit(key, dst, engine):
-            res = sb.tile([P, KP], F32, name="res_" + key, tag="res", bufs=RES_BUFS)
-            copy_on(engine, res[:], accs[key][:])
+        def dw_passes(s, side, g):
+            for t in range(PACK):
+                dw_pass(s, side, t, g)
+
+        def store(total, dst, engine):
+            res = sb.tile([P, dst.shape[1]], F32, name="result", tag="result", bufs=6)
+            copy(engine, res[:], total)
             nc.sync.dma_start(out=dst, in_=res[:])
 
-        def dx_neighbour(g, i):
-            acc = new_acc("n%d%d" % (g, i), 3 + i)
-            for h in range(HH):
-                mm(acc, "b%d%d" % (HH * g + h, i // 2), i % 2, "w1n%d" % h, h == 0, h == HH - 1)
+        def store_dx(g):
+            for n in (1, 2, 3, 4, 0):
+                store(sums["dx", g, n][:], out_0[g * P:(g + 1) * P, n, :], SCALAR)
 
-        def emit_neighbour(g, i, engine):
-            emit("n%d%d" % (g, i), out_0[g * P:(g + 1) * P, 1 + i, :], engine)
+        dw_rows = out_1.rearrange("(s w t) f -> s t w f", s=HALVES, t=PACK)
+        dw_cols = {"a": slice(0, F), "n": slice(F, 2 * F)}
 
-        def dx_anchor(g):
-            acc = new_acc("a%d" % g, 7)
-            mm(acc, "grad%d" % (g // 2), g % 2, "w0", True, False)
-            for h in range(HH):
-                for i in range(NB):
-                    mm(acc, "b%d%d" % (HH * g + h, i // 2), i % 2, "w1a%d" % h, False, h == HH - 1 and i == NB - 1)
+        def store_dw(s, side, t, engine):
+            store(sums[s, side, t][:], dw_rows[s, t, :, dw_cols[side]], engine)
 
-        def emit_anchor(g, engine):
-            emit("a%d" % g, out_0[g * P:(g + 1) * P, 0, :], engine)
+        load_w2()
+        load_grad(0)
+        load_tanh(0)
+        load_tanh(1)
+        load_w1(0)
+        load_grad(1)
+        load_w0()
+        load_tanh(2)
+        load_w1(1)
+        load_tanh(3)
 
-        dw_rows = out_1.rearrange("(h m t) f -> h t m f", h=HH, t=PACK)
+        weave_w2(0, "woven", 4)
+        turn_grad(0, DX_BANK)
+        fetch_grad(0)
+        weave_w2(1, "gpsimd", 1)
+        quantize("w20")
+        quantize("grad0")
+        square(0)
+        dh_pass(0)
+        quantize("w21")
+        dh_pass(1, DX_BANK + 2)
+        square(1)
+        make_dz(0)
+        load_x(0)
+        load_tanh(4)
+        turn_dz(0)
+        fetch_dz(0, 0, SCALAR)
+        weave_on_gpsimd("w1n0")
+        make_dz(1)
+        fetch_dz(0, 1, VECTOR)
+        weave("w0", SCALAR)
+        quantize("feat0")
+        dh_pass(2)
+        turn_dz(1)
+        turn_grad(1, DX_BANK + 3)
+        weave("w1a0", VECTOR)
+        square(2)
+        fetch_grad(1)
+        fetch_dz(1, 0, SCALAR)
+        quantize("w0")
+        quantize("w1a0")
+        quantize("w1n0")
+        dx_passes(0)
+        for g in (1, 2):
+            load_x(g)
+            load_tanh(4 + g)
 
-        def dw_pass(h, side, t, g, bank):
-            key = "w%d%s%d" % (h, side, t)
-            if g == 0:
-                new_acc(key, bank)
-            mm(accs[key], "a%d" % (HH * g + h), t, "x%s%d" % (side, g), g == 0, g == G - 1)
-
-        def emit_dw(h, side, t, engine):
-            first = 0 if side == "a" else F
-            emit("w%d%s%d" % (h, side, t), dw_rows[h, t, :, first:first + F], engine)
-
-        def prepare(key, engine):
-            if key[0] == "a":
-                weave_dz(int(key[1]), engine)
-            elif key[:2] == "xa":
-                weave_anchor(int(key[2]), engine)
+        gpsimd_work = ["w1n1"] + ["xn%d" % g for g in range(BLOCKS)] + ["xa0"]
+        for c in range(2, CHUNKS):
+            operand = gpsimd_work[c - 2]
+            weave_on_gpsimd(operand)
+            make_dz(c)
+            fetch_dz(c - 1, 1, VECTOR)
+            quantize("feat%d" % (c - 1))
+            if c == 2:
+                weave("w1a1", SCALAR)
+            if c % 2 == 0:
+                for ahead in range(c + 1, min(c + 3, CHUNKS)):
+                    square(ahead)
             else:
-                weave(key, engine)
-
-        def finish(key):
-            quantize(key, E5 if key[0] == "a" else E4)
-
-
-        for key in LOADS:
-            if key[0] == "w" or key[:2] == "xn":
-                load_rows(key)
-            elif key[0] == "g":
-                load_grad(int(key[-1]))
-            elif key[0] == "x":
-                load_anchor(int(key[-1]))
+                store_dx(c // 2 - 1)
+            if c + 1 < CHUNKS:
+                dh_pass(c + 1)
+            turn_dz(c)
+            if c == 2:
+                quantize("grad1")
+                quantize("w1a1")
+                quantize(operand)
+                dx_passes(c - 1)
+                load_x(3)
+                load_tanh(7)
             else:
-                load_tanh(int(key[-1]))
+                dx_passes(c - 1)
+                quantize(operand)
+            fetch_dz(c, 0, SCALAR)
+        last = CHUNKS - 1
+        fetch_dz(last, 1, SCALAR)
 
-        def item(key, engine):
-            prepare(key, engine)
-            finish(key)
-
-        def front(k):
-            square(k)
-            dh_product(k)
-            make_dz(k)
-
-        def back(k, e0, e1):
-            turn_dz(k)
-            fetch_dz(k, 0, e0)
-            quantize_b(k, 0)
-            fetch_dz(k, 1, e1)
-            quantize_b(k, 1)
-
-        def rows(g, engines):
-            for i in range(NB):
-                dx_neighbour(g, i)
-                emit_neighbour(g, i, engines[i])
-            dx_anchor(g)
-            emit_anchor(g, engines[4])
-
-        def block(h, side, first, engines):
-            for t in range(PACK):
-                for g in range(G):
-                    dw_pass(h, side, t, g, first + t)
-                emit_dw(h, side, t, engines[t])
-
-        weave_w2(0)
-        turn_grad(0, "S")
-        quantize("w20", E4)
-        quantize("grad0", E5)
-        front(0)
-        weave_w2(1)
-        quantize("w21", E4)
-        for step in ORDER.split():
-            a = step.split(":")
-            if a[0] == "f":
-                front(int(a[1]))
-            elif a[0] == "b":
-                back(int(a[1]), a[2][0], a[2][1])
-            elif a[0] == "i":
-                item(a[1], a[2])
-            elif a[0] == "q":
-                finish(a[1])
-            elif a[0] == "r":
-                rows(int(a[1]), a[2])
-            elif a[0] == "g":
-                turn_grad(1, "S")
-                quantize("grad1", E5)
-            elif a[0] == "l":
-                if a[1][0] == "t":
-                    load_tanh(int(a[1][1]))
-                elif a[1][1] == "n":
-                    load_rows(a[1])
-                else:
-                    load_anchor(int(a[1][2]))
-            else:
-                block(int(a[1]), a[2], int(a[3]), a[4])
+        weave_tokens(4, SCALAR)
+        quantize("feat%d" % last)
+        weave_tokens(0, VECTOR)
+        dx_passes(last)
+        weave_tokens(2, VECTOR)
+        quantize("tok0")
+        quantize("tok2")
+        dw_passes(0, "n", 0)
+        dw_passes(0, "n", 1)
+        store_dx(BLOCKS - 1)
+        weave_tokens(6, VECTOR)
+        quantize("tok4")
+        quantize("tok6")
+        dw_passes(0, "n", 2)
+        dw_passes(0, "n", 3)
+        weave_anchor(1, SCALAR)
+        weave_anchor(2, VECTOR)
+        weave_anchor(3, SCALAR)
+        quantize("xa1")
+        weave_tokens(1, VECTOR)
+        quantize("xa2")
+        quantize("xa3")
+        for g in range(BLOCKS):
+            dw_passes(0, "a", g)
+        for t in range(PACK):
+            store_dw(0, "n", t, SCALAR)
+        weave_tokens(3, VECTOR)
+        quantize("tok1")
+        weave_tokens(5, SCALAR)
+        quantize("tok3")
+        weave_tokens(7, VECTOR)
+        quantize("tok5")
+        quantize("tok7")
+        for g in range(BLOCKS):
+            dw_passes(1, "n", g)
+        for t in range(PACK):
+            store_dw(0, "a", t, SCALAR)
+        for t in range(PACK):
+            store_dw(1, "n", t, SCALAR if t % 2 else VECTOR)
+        for t in range(PACK):
+            for g in range(BLOCKS):
+                dw_pass(1, "a", t, g)
+            if t < PACK - 1:
+                store_dw(1, "a", t, SCALAR if t % 2 else VECTOR)
+        for n in range(2):
+            cols = slice(n * F // 2, (n + 1) * F // 2)
+            store(sums[1, "a", PACK - 1][:, cols], dw_rows[1, PACK - 1, :, cols], SCALAR)

@@ -148,7 +148,7 @@ def tile_attention_pa_v_kernel(tc, x, W1, W2, W0, interact, grad_out, out_0, out
             turned["grad", pair] = t
 
         def fetch_grad(pair):
-            t = new_woven("grad%d" % pair, tag="woven_grad", bufs=2, width=HALF)
+            t = new_woven("grad%d" % pair, tag="woven_feat", bufs=2, width=HALF)
             nc.scalar.copy(out=t[:].bitcast(F32).rearrange("p (g b u) -> p g b u", g=2, u=2),
                            in_=turned["grad", pair][:].rearrange("p (g u) b -> p g b u", u=2))
 
@@ -213,7 +213,7 @@ def tile_attention_pa_v_kernel(tc, x, W1, W2, W0, interact, grad_out, out_0, out
                 dw_pass(s, side, t, g)
 
         def store(total, dst, engine):
-            res = sb.tile([P, dst.shape[1]], F32, name="result", tag="result", bufs=6)
+            res = sb.tile([P, dst.shape[1]], F32, name="result", tag="result", bufs=2 * (NB + 1))
             copy(engine, res[:], total)
             nc.sync.dma_start(out=dst, in_=res[:])
 
@@ -232,9 +232,9 @@ def tile_attention_pa_v_kernel(tc, x, W1, W2, W0, interact, grad_out, out_0, out
         load_tanh(0)
         load_tanh(1)
         load_w1(0)
-        load_grad(1)
         load_w0()
         load_tanh(2)
+        load_grad(1)
         load_w1(1)
         load_tanh(3)
 
@@ -284,8 +284,7 @@ def tile_attention_pa_v_kernel(tc, x, W1, W2, W0, interact, grad_out, out_0, out
             if c == 2:
                 weave("w1a1", SCALAR)
             if c % 2 == 0:
-                for ahead in range(c + 1, min(c + 3, CHUNKS)):
-                    square(ahead)
+                square(c + 1)
             else:
                 store_dx(c // 2 - 1)
             if c + 1 < CHUNKS:
@@ -302,6 +301,8 @@ def tile_attention_pa_v_kernel(tc, x, W1, W2, W0, interact, grad_out, out_0, out
                 dx_passes(c - 1)
                 quantize(operand)
             fetch_dz(c, 0, SCALAR)
+            if c % 2 == 0 and c + 2 < CHUNKS:
+                square(c + 2)
         last = CHUNKS - 1
         fetch_dz(last, 1, SCALAR)
 

@@ -12,6 +12,7 @@ HALF = WIDE // 2
 BLOCKS = B // P
 HALVES = H // KP
 CHUNKS = BLOCKS * HALVES
+EARLY = 2
 
 DH_BANK, TURN_BANK, DX_BANK = 0, 1, 3
 DW_BANKS = {"n": 0, "a": 4}
@@ -63,9 +64,17 @@ def tile_attention_pa_v_kernel(tc, x, W1, W2, W0, interact, grad_out, out_0, out
             raw["w1a%d" % s], raw["w1n%d" % s] = t[:, :, 0:F], t[:, :, F:2 * F]
 
         def load_x(g):
-            t = load_rows("x%d" % g, x[g * P:(g + 1) * P])
-            raw["xn%d" % g] = t[:, 1:, :]
-            raw["xa%d" % g] = t[:, 0, :]
+            first = 1 if g < EARLY else 0
+            t = load_rows("x%d" % g, x[g * P:(g + 1) * P, first:, :])
+            raw["xn%d" % g] = t[:, 1 - first:, :]
+            if g >= EARLY:
+                raw["xa%d" % g] = t[:, 0, :]
+
+        def load_early_anchors():
+            t = sb.tile([P, EARLY, F], BF16, name="raw_anchors", align_bytes=64)
+            nc.sync.dma_start(out=t[:], in_=x[0:EARLY * P, 0, :].rearrange("(g p) f -> p g f", p=P))
+            for g in range(EARLY):
+                raw["xa%d" % g] = t[:, g, :]
 
         def load_grad(pair):
             t = sb.tile([P, 2, F], BF16, name="raw_grad%d" % pair, align_bytes=64)
@@ -103,8 +112,8 @@ def tile_attention_pa_v_kernel(tc, x, W1, W2, W0, interact, grad_out, out_0, out
             name = "xa%d" % g
             copy(engine, new_woven(name)[:].rearrange("p (n j) -> p n j", j=PACK), side_by_side(name))
 
-        def weave_on_gpsimd(name):
-            t = new_woven(name, tag="gpsimd", bufs=1)
+        def weave_on_gpsimd(name, tag="gpsimd", bufs=1):
+            t = new_woven(name, tag=tag, bufs=bufs)
             nc.gpsimd.tensor_scalar(out=t[:].rearrange("p (n j) -> p n j", j=PACK),
                                     in0=side_by_side(name),
                                     scalar1=1.0, scalar2=0.0, op0=ALU.mult, op1=ALU.add)
@@ -217,9 +226,9 @@ def tile_attention_pa_v_kernel(tc, x, W1, W2, W0, interact, grad_out, out_0, out
             copy(engine, res[:], total)
             nc.sync.dma_start(out=dst, in_=res[:])
 
-        def store_dx(g):
+        def store_dx(g, first_engine):
             for n in (1, 2, 3, 4, 0):
-                store(sums["dx", g, n][:], out_0[g * P:(g + 1) * P, n, :], SCALAR)
+                store(sums["dx", g, n][:], out_0[g * P:(g + 1) * P, n, :], first_engine if n == 1 else SCALAR)
 
         dw_rows = out_1.rearrange("(s w t) f -> s t w f", s=HALVES, t=PACK)
         dw_cols = {"a": slice(0, F), "n": slice(F, 2 * F)}
@@ -227,6 +236,7 @@ def tile_attention_pa_v_kernel(tc, x, W1, W2, W0, interact, grad_out, out_0, out
         def store_dw(s, side, t, engine):
             store(sums[s, side, t][:], dw_rows[s, t, :, dw_cols[side]], engine)
 
+        load_early_anchors()
         load_w2()
         load_grad(0)
         load_tanh(0)
@@ -238,6 +248,9 @@ def tile_attention_pa_v_kernel(tc, x, W1, W2, W0, interact, grad_out, out_0, out
         load_w1(1)
         load_tanh(3)
 
+        weave_anchor(0, VECTOR)
+        weave_anchor(1, SCALAR)
+        quantize("xa0")
         weave_w2(0, "woven", 4)
         turn_grad(0, DX_BANK)
         fetch_grad(0)
@@ -247,6 +260,7 @@ def tile_attention_pa_v_kernel(tc, x, W1, W2, W0, interact, grad_out, out_0, out
         square(0)
         dh_pass(0)
         quantize("w21")
+        quantize("xa1")
         dh_pass(1, DX_BANK + 2)
         square(1)
         make_dz(0)
@@ -274,65 +288,68 @@ def tile_attention_pa_v_kernel(tc, x, W1, W2, W0, interact, grad_out, out_0, out
             load_x(g)
             load_tanh(4 + g)
 
-        gpsimd_work = ["w1n1"] + ["xn%d" % g for g in range(BLOCKS)] + ["xa0"]
+        gpsimd_work = ["w1n1"] + ["xn%d" % g for g in range(BLOCKS)]
+        last = CHUNKS - 1
         for c in range(2, CHUNKS):
-            operand = gpsimd_work[c - 2]
-            weave_on_gpsimd(operand)
+            if c < last:
+                weave_on_gpsimd(gpsimd_work[c - 2])
+            else:
+                weave_on_gpsimd("xa2", tag="woven_feat", bufs=2)
             make_dz(c)
-            fetch_dz(c - 1, 1, VECTOR)
+            if c % 2:
+                fetch_dz(c - 1, 1, SCALAR)
+                store_dx(c // 2 - 1, VECTOR)
+            else:
+                fetch_dz(c - 1, 1, VECTOR)
             quantize("feat%d" % (c - 1))
             if c == 2:
                 weave("w1a1", SCALAR)
             if c % 2 == 0:
                 square(c + 1)
-            else:
-                store_dx(c // 2 - 1)
             if c + 1 < CHUNKS:
                 dh_pass(c + 1)
             turn_dz(c)
             if c == 2:
                 quantize("grad1")
                 quantize("w1a1")
-                quantize(operand)
+                quantize(gpsimd_work[0])
                 dx_passes(c - 1)
                 load_x(3)
                 load_tanh(7)
             else:
                 dx_passes(c - 1)
-                quantize(operand)
+                if c + 1 < last:
+                    quantize(gpsimd_work[c - 2])
             fetch_dz(c, 0, SCALAR)
             if c % 2 == 0 and c + 2 < CHUNKS:
                 square(c + 2)
-        last = CHUNKS - 1
         fetch_dz(last, 1, SCALAR)
 
+        weave_tokens(0, VECTOR)
         weave_tokens(4, SCALAR)
         quantize("feat%d" % last)
-        weave_tokens(0, VECTOR)
         dx_passes(last)
         weave_tokens(2, VECTOR)
         quantize("tok0")
         quantize("tok2")
         dw_passes(0, "n", 0)
         dw_passes(0, "n", 1)
-        store_dx(BLOCKS - 1)
+        store_dx(BLOCKS - 1, SCALAR)
         weave_tokens(6, VECTOR)
         quantize("tok4")
+        quantize("xn3")
         quantize("tok6")
         dw_passes(0, "n", 2)
         dw_passes(0, "n", 3)
-        weave_anchor(1, SCALAR)
-        weave_anchor(2, VECTOR)
         weave_anchor(3, SCALAR)
-        quantize("xa1")
-        weave_tokens(1, VECTOR)
         quantize("xa2")
+        weave_tokens(1, VECTOR)
+        weave_tokens(3, VECTOR)
         quantize("xa3")
         for g in range(BLOCKS):
             dw_passes(0, "a", g)
         for t in range(PACK):
             store_dw(0, "n", t, SCALAR)
-        weave_tokens(3, VECTOR)
         quantize("tok1")
         weave_tokens(5, SCALAR)
         quantize("tok3")

from contextlib import ExitStack

import concourse.mybir as mybir
from concourse.masks import make_identity

B, NB, F, H = 512, 4, 512, 1024
P = 128
PACK = 4
KP = P * PACK
WIDE = KP * PACK
HALF = WIDE // 2
BLOCKS = B // P
HALVES = H // KP
CHUNKS = BLOCKS * HALVES
EARLY = 2

DH_BANK, TURN_BANK, DX_BANK = 0, 1, 3
DW_BANKS = {"n": 0, "a": 4}

F32 = mybir.dt.float32
BF16 = mybir.dt.bfloat16
U32 = mybir.dt.uint32
U8 = mybir.dt.uint8
E4 = mybir.dt.float8_e4m3fn_x4
E5 = mybir.dt.float8_e5m2_x4
ALU = mybir.AluOpType
ACT = mybir.ActivationFunctionType
SCALAR, VECTOR = "scalar", "vector"

FLOPS = 2 * B * F * (H + F) + 2 * 2 * B * NB * H * 2 * F


def tile_attention_pa_v_kernel(tc, x, W1, W2, W0, interact, grad_out, out_0, out_1):
    nc = tc.nc
    with ExitStack() as ctx:
        sb = ctx.enter_context(tc.tile_pool(name="sb", bufs=1))
        psum = ctx.enter_context(tc.psum_pool(name="psum", bufs=1))
        ctx.enter_context(tc.manual_schedule())

        ident = sb.tile([P, P], F32, name="ident")
        make_identity(nc, ident[:])

        raw, woven, mx = {}, {}, {}
        tanh, squares, neg_dh, dz, turned, sums = {}, {}, {}, {}, {}, {}

        def bank(name, number, shape):
            return psum.tile(shape, F32, name=name, tag="bank%d" % number)

        def load_rows(name, source):
            t = sb.tile([P] + list(source.shape[1:]), BF16, name="raw_" + name, tag="rows", bufs=4, align_bytes=64)
            nc.sync.dma_start(out=t[:], in_=source)
            return t

        def load_w2():
            t = load_rows("w2", W2.rearrange("(p j) h -> p j h", j=PACK))
            for s in range(HALVES):
                raw["w2%d" % s] = t[:, :, s * KP:(s + 1) * KP]

        def load_w0():
            raw["w0"] = load_rows("w0", W0.rearrange("(p j) f -> p j f", j=PACK))[:]

        def load_w1(s):
            t = load_rows("w1%d" % s, W1.rearrange("(s p j) f -> s p j f", s=HALVES, j=PACK)[s])
            raw["w1a%d" % s], raw["w1n%d" % s] = t[:, :, 0:F], t[:, :, F:2 * F]

        def load_x(g):
            first = 1 if g < EARLY else 0
            t = load_rows("x%d" % g, x[g * P:(g + 1) * P, first:, :])
            raw["xn%d" % g] = t[:, 1 - first:, :]
            if g >= EARLY:
                raw["xa%d" % g] = t[:, 0, :]

        def load_early_anchors():
            t = sb.tile([P, EARLY, F], BF16, name="raw_anchors", align_bytes=64)
            nc.sync.dma_start(out=t[:], in_=x[0:EARLY * P, 0, :].rearrange("(g p) f -> p g f", p=P))
            for g in range(EARLY):
                raw["xa%d" % g] = t[:, g, :]

        def load_grad(pair):
            t = sb.tile([P, 2, F], BF16, name="raw_grad%d" % pair, align_bytes=64)
            rows = grad_out[2 * pair * P:2 * (pair + 1) * P]
            nc.sync.dma_start(out=t[:], in_=rows.rearrange("(g p) f -> p g f", p=P))
            raw["grad%d" % pair] = t

        def load_tanh(c):
            g, s = divmod(c, HALVES)
            t = sb.tile([P, NB, KP], F32, name="tanh%d" % c, tag="tanh", bufs=4, align_bytes=64)
            nc.sync.dma_start(out=t[:], in_=interact[g * P:(g + 1) * P, :, s * KP:(s + 1) * KP])
            tanh[c] = t

        def new_woven(name, tag="woven", bufs=4, width=WIDE):
            t = sb.tile([P, width], BF16, name="woven_" + name, tag=tag, bufs=bufs, align_bytes=64)
            woven[name] = t
            return t

        def copy(engine, out, in_):
            if engine == SCALAR:
                nc.scalar.copy(out=out, in_=in_)
            else:
                nc.vector.tensor_copy(out=out, in_=in_)

        def weave(name, engine):
            copy(engine, new_woven(name)[:].rearrange("p (n r j) -> p n j r", r=4, j=PACK),
                 raw[name].rearrange("p j (n r) -> p n j r", r=4))

        def side_by_side(name):
            if name.startswith("xa"):
                return raw[name].unsqueeze(2).to_broadcast([P, F, NB])
            return raw[name].rearrange("p j n -> p n j")

        def weave_anchor(g, engine):
            name = "xa%d" % g
            copy(engine, new_woven(name)[:].rearrange("p (n j) -> p n j", j=PACK), side_by_side(name))

        def weave_on_gpsimd(name, tag="gpsimd", bufs=1):
            t = new_woven(name, tag=tag, bufs=bufs)
            nc.gpsimd.tensor_scalar(out=t[:].rearrange("p (n j) -> p n j", j=PACK),
                                    in0=side_by_side(name),
                                    scalar1=1.0, scalar2=0.0, op0=ALU.mult, op1=ALU.add)

        def weave_w2(s, tag, bufs):
            name = "w2%d" % s
            t = new_woven(name, tag=tag, bufs=bufs)
            for u in range(2):
                nc.vector.tensor_scalar(
                    out=t[:, u * HALF:(u + 1) * HALF].rearrange("p (w e j) -> p w j e", e=2, j=PACK),
                    in0=raw[name].rearrange("p j (w u e) -> p u w j e", u=2, e=2)[:, u],
                    scalar1=-1.0, scalar2=None, op0=ALU.mult)

        def weave_tokens(c, engine):
            copy(engine, new_woven("tok%d" % c)[:].rearrange("p (u e w i) -> p u w i e", u=2, e=2, i=NB),
                 dz[c][:].rearrange("p (u i w e) -> p u w i e", u=2, i=NB, e=2))

        def quantize(name):
            src = woven[name]
            words = src.shape[1] // PACK
            fmt = E4 if name[0] in "wx" else E5
            tag, bufs = ("feat", 4) if name.startswith("feat") else (name, 1)
            codes = sb.tile([P, words], U32, name="codes_" + name, tag=tag + "_codes", bufs=bufs, align_bytes=64)
            scales = sb.tile([P, words], U8, name="scales_" + name, tag=tag + "_scales", bufs=bufs, align_bytes=64)
            nc.vector.quantize_mx(out=codes[:].bitcast(fmt), scales=scales[:], in_=src[:])
            mx[name] = (codes, scales, fmt)

        def mx_pass(out, left, block, right, start, stop):
            left_codes, left_scales, left_fmt = mx[left]
            right_codes, right_scales, right_fmt = mx[right]
            cols = slice(block * P, (block + 1) * P)
            nc.tensor.matmul_mx(out=out[:], lhsT=left_codes[:, cols].bitcast(left_fmt), lhsT_scale=left_scales[:, cols],
                                rhs=right_codes[:].bitcast(right_fmt), rhs_scale=right_scales[:], start=start, stop=stop)

        def turn_grad(pair, number):
            words = raw["grad%d" % pair][:].rearrange("p g f -> p (g f)").bitcast(F32)
            t = bank("turn_grad%d" % pair, number, [P, 4, P])
            for n in range(4):
                g, u = divmod(n, 2)
                nc.tensor.transpose(t[:, n, :], words[:, 2 * P * g + u:2 * P * (g + 1):2], ident[:])
            turned["grad", pair] = t

        def fetch_grad(pair):
            t = new_woven("grad%d" % pair, tag="woven_feat", bufs=2, width=HALF)
            nc.scalar.copy(out=t[:].bitcast(F32).rearrange("p (g b u) -> p g b u", g=2, u=2),
                           in_=turned["grad", pair][:].rearrange("p (g u) b -> p g b u", u=2))

        def square(c):
            t = sb.tile([P, WIDE], F32, name="square%d" % c, tag="square", bufs=2, align_bytes=64)
            nc.scalar.activation(out=t[:], in_=tanh[c][:].rearrange("p i h -> p (i h)"), func=ACT.Square)
            squares[c] = t

        def dh_pass(c, number=DH_BANK):
            g, s = divmod(c, HALVES)
            neg_dh[c] = bank("neg_dh%d" % c, number, [P, KP])
            mx_pass(neg_dh[c], "grad%d" % (g // 2), g % 2, "w2%d" % s, True, True)

        def make_dz(c):
            t = sb.tile([P, WIDE], BF16, name="dz%d" % c, tag="dz", bufs=CHUNKS, align_bytes=64)
            for u in range(2):
                factor = neg_dh[c][:, u * 2 * P:(u + 1) * 2 * P].rearrange("p (w e) -> p w e", e=2)
                nc.vector.scalar_tensor_tensor(
                    out=t[:, u * HALF:(u + 1) * HALF].rearrange("p (i w e) -> p i w e", i=NB, e=2),
                    in0=squares[c][:].rearrange("p (i w u e) -> p u i w e", i=NB, u=2, e=2)[:, u], scalar=1.0,
                    in1=factor.unsqueeze(1).to_broadcast([P, NB, P, 2]),
                    op0=ALU.subtract, op1=ALU.mult)
            dz[c] = t

        def turn_dz(c):
            words = dz[c][:].bitcast(F32).rearrange("p (u i w) -> p u i w", u=2, i=NB)
            for pair in range(2):
                t = bank("turn%d_%d" % (c, pair), TURN_BANK + pair, [P, 4, P])
                for n in range(4):
                    i, u = divmod(n, 2)
                    nc.tensor.transpose(t[:, n, :], words[:, u, 2 * pair + i, :], ident[:])
                turned[c, pair] = t

        def fetch_dz(c, pair, engine):
            name = "feat%d" % c
            if pair == 0:
                new_woven(name, tag="woven_feat", bufs=2)
            part = woven[name][:, pair * HALF:(pair + 1) * HALF]
            copy(engine, part.bitcast(F32).rearrange("p (i b u) -> p i b u", i=2, u=2),
                 turned[c, pair][:].rearrange("p (i u) b -> p i b u", u=2))

        def dx_passes(c):
            g, s = divmod(c, HALVES)
            last = s == HALVES - 1
            for i in range(NB):
                if s == 0:
                    sums["dx", g, 1 + i] = bank("dx%d_%d" % (g, 1 + i), DX_BANK + i, [P, KP])
                mx_pass(sums["dx", g, 1 + i], "feat%d" % c, i, "w1n%d" % s, s == 0, last)
            if s == 0:
                sums["dx", g, 0] = bank("dx%d_0" % g, DX_BANK + NB, [P, KP])
                mx_pass(sums["dx", g, 0], "grad%d" % (g // 2), g % 2, "w0", True, False)
            for i in range(NB):
                mx_pass(sums["dx", g, 0], "feat%d" % c, i, "w1a%d" % s, False, last and i == NB - 1)

        def dw_pass(s, side, t, g):
            if g == 0:
                sums[s, side, t] = bank("dw%d%s%d" % (s, side, t), DW_BANKS[side] + t, [P, KP])
            mx_pass(sums[s, side, t], "tok%d" % (HALVES * g + s), t, "x%s%d" % (side, g), g == 0, g == BLOCKS - 1)

        def dw_passes(s, side, g):
            for t in range(PACK):
                dw_pass(s, side, t, g)

        def store(total, dst, engine):
            res = sb.tile([P, dst.shape[1]], F32, name="result", tag="result", bufs=2 * (NB + 1))
            copy(engine, res[:], total)
            nc.sync.dma_start(out=dst, in_=res[:])

        def store_dx(g, first_engine):
            for n in (1, 2, 3, 4, 0):
                store(sums["dx", g, n][:], out_0[g * P:(g + 1) * P, n, :], first_engine if n == 1 else SCALAR)

        dw_rows = out_1.rearrange("(s w t) f -> s t w f", s=HALVES, t=PACK)
        dw_cols = {"a": slice(0, F), "n": slice(F, 2 * F)}

        def store_dw(s, side, t, engine):
            store(sums[s, side, t][:], dw_rows[s, t, :, dw_cols[side]], engine)

        load_early_anchors()
        load_w2()
        load_grad(0)
        load_tanh(0)
        load_tanh(1)
        load_w1(0)
        load_w0()
        load_tanh(2)
        load_grad(1)
        load_w1(1)
        load_tanh(3)

        weave_anchor(0, VECTOR)
        weave_anchor(1, SCALAR)
        quantize("xa0")
        weave_w2(0, "woven", 4)
        turn_grad(0, DX_BANK)
        fetch_grad(0)
        weave_w2(1, "gpsimd", 1)
        quantize("w20")
        quantize("grad0")
        square(0)
        dh_pass(0)
        quantize("w21")
        quantize("xa1")
        dh_pass(1, DX_BANK + 2)
        square(1)
        make_dz(0)
        load_x(0)
        load_tanh(4)
        turn_dz(0)
        fetch_dz(0, 0, SCALAR)
        weave_on_gpsimd("w1n0")
        make_dz(1)
        fetch_dz(0, 1, VECTOR)
        weave("w0", SCALAR)
        quantize("feat0")
        dh_pass(2)
        turn_dz(1)
        turn_grad(1, DX_BANK + 3)
        weave("w1a0", VECTOR)
        square(2)
        fetch_grad(1)
        fetch_dz(1, 0, SCALAR)
        quantize("w0")
        quantize("w1a0")
        quantize("w1n0")
        dx_passes(0)
        for g in (1, 2):
            load_x(g)
            load_tanh(4 + g)

        gpsimd_work = ["w1n1"] + ["xn%d" % g for g in range(BLOCKS)]
        last = CHUNKS - 1
        for c in range(2, CHUNKS):
            if c < last:
                weave_on_gpsimd(gpsimd_work[c - 2])
            else:
                weave_on_gpsimd("xa2", tag="woven_feat", bufs=2)
            make_dz(c)
            if c % 2:
                fetch_dz(c - 1, 1, SCALAR)
                store_dx(c // 2 - 1, VECTOR)
            else:
                fetch_dz(c - 1, 1, VECTOR)
            quantize("feat%d" % (c - 1))
            if c == 2:
                weave("w1a1", SCALAR)
            if c % 2 == 0:
                square(c + 1)
            if c + 1 < CHUNKS:
                dh_pass(c + 1)
            turn_dz(c)
            if c == 2:
                quantize("grad1")
                quantize("w1a1")
                quantize(gpsimd_work[0])
                dx_passes(c - 1)
                load_x(3)
                load_tanh(7)
            else:
                dx_passes(c - 1)
                if c + 1 < last:
                    quantize(gpsimd_work[c - 2])
            fetch_dz(c, 0, SCALAR)
            if c % 2 == 0 and c + 2 < CHUNKS:
                square(c + 2)
        fetch_dz(last, 1, SCALAR)

        weave_tokens(0, VECTOR)
        weave_tokens(4, SCALAR)
        quantize("feat%d" % last)
        dx_passes(last)
        weave_tokens(2, VECTOR)
        quantize("tok0")
        quantize("tok2")
        dw_passes(0, "n", 0)
        dw_passes(0, "n", 1)
        store_dx(BLOCKS - 1, SCALAR)
        weave_tokens(6, VECTOR)
        quantize("tok4")
        quantize("xn3")
        quantize("tok6")
        dw_passes(0, "n", 2)
        dw_passes(0, "n", 3)
        weave_anchor(3, SCALAR)
        quantize("xa2")
        weave_tokens(1, VECTOR)
        weave_tokens(3, VECTOR)
        quantize("xa3")
        for g in range(BLOCKS):
            dw_passes(0, "a", g)
        for t in range(PACK):
            store_dw(0, "n", t, SCALAR)
        quantize("tok1")
        weave_tokens(5, SCALAR)
        quantize("tok3")
        weave_tokens(7, VECTOR)
        quantize("tok5")
        quantize("tok7")
        for g in range(BLOCKS):
            dw_passes(1, "n", g)
        for t in range(PACK):
            store_dw(0, "a", t, SCALAR)
        for t in range(PACK):
            store_dw(1, "n", t, SCALAR if t % 2 else VECTOR)
        for t in range(PACK):
            for g in range(BLOCKS):
                dw_pass(1, "a", t, g)
            if t < PACK - 1:
                store_dw(1, "a", t, SCALAR if t % 2 else VECTOR)
        for n in range(2):
            cols = slice(n * F // 2, (n + 1) * F // 2)
            store(sums[1, "a", PACK - 1][:, cols], dw_rows[1, PACK - 1, :, cols], SCALAR)
